import numpy as np
import ml_dtypes


def mxq(x, axis, fmt="e4m3"):
    dtype, down = {"e4m3": (ml_dtypes.float8_e4m3fn, 7), "e5m2": (ml_dtypes.float8_e5m2, 14)}[fmt]
    v = np.moveaxis(np.asarray(x, np.float32).astype(ml_dtypes.bfloat16).astype(np.float64), axis, -1)
    blocks = v.reshape(v.shape[:-1] + (-1, 32))
    amax = np.abs(blocks).max(-1, keepdims=True)
    byte = np.maximum(np.where(amax > 0, np.frexp(amax)[1] - 1 + 127, 0) - down, 1)
    scale = np.exp2(byte - 127.0)
    codes = (blocks / scale).astype(np.float32).astype(dtype).astype(np.float64)
    return np.moveaxis((codes * scale).reshape(v.shape), -1, axis)


WIDE = False


def mx_kscale(k):
    if not WIDE:
        return np.ones(k)
    levels = np.array([10, -10, 5, -5, 0])
    if k % 512:
        return np.exp2(np.random.permutation(np.resize(levels, k // 32))).repeat(32)
    a = np.empty((k // 512, 16))
    for p in range(k // 512):
        a[p, :8] = np.random.permutation(np.resize(levels, 8))
        for g in range(8):
            far = levels[np.abs(levels - a[p, g]) >= 10]
            a[p, g + 8] = far[np.random.randint(len(far))]
    return np.exp2(a.ravel()).repeat(32)


BF16 = ml_dtypes.bfloat16


def bf(x):
    return np.asarray(x, np.float32).astype(BF16)


def f64(x):
    return np.asarray(x).astype(np.float64)


B, NH, HD, H, W = 1, 3, 512, 64, 64
NEG_INF = -1e9


def setup_inputs():
    s = mx_kscale(HD)[None, None, :, None, None]
    a = 1.3 / HD ** 0.25
    return {"q": bf(np.random.standard_normal((B, NH, HD, H, W)) * a * s),
            "k": bf(np.random.standard_normal((B, NH, HD, H, W)) * a / s)}


def core(q, k):
    qq = mxq(f64(q), 2, "e4m3")
    kq = mxq(f64(k), 2, "e4m3")
    e_h = (qq.transpose(0, 1, 4, 3, 2) @ kq.transpose(0, 1, 4, 2, 3)).transpose(0, 1, 3, 2, 4)
    e_h = np.where(np.eye(H, dtype=bool)[:, None, :], NEG_INF, e_h)
    e_w = qq.transpose(0, 1, 3, 4, 2) @ kq.transpose(0, 1, 3, 2, 4)
    e = np.concatenate([e_h, e_w], axis=-1)
    p = np.exp(e - e.max(-1, keepdims=True))
    return p / p.sum(-1, keepdims=True)


def e4m3fn_bytes(y):
    return np.clip(np.asarray(y, np.float64), -448.0, 448.0).astype(np.float32).astype(ml_dtypes.float8_e4m3fn).view(np.uint8)


Y_SCALE = 12000.0


def reference(q, k):
    out = core(q, k)
    return out, e4m3fn_bytes(out * Y_SCALE)

@@ -1,0 +1,304 @@
+from contextlib import ExitStack
+
+import concourse.mybir as mybir
+from concourse.masks import make_identity
+
+NH, HD, H, W = 3, 512, 64, 64
+FLOPS = 2 * NH * H * W * (H + W) * HD
+
+F32 = mybir.dt.float32
+BF16 = mybir.dt.bfloat16
+I32 = mybir.dt.int32
+U8 = mybir.dt.uint8
+FP8X4 = mybir.dt.float8_e4m3fn_x4
+FP8 = mybir.dt.float8_e4m3fn
+ALU = mybir.AluOpType
+ACT = mybir.ActivationFunctionType
+AX = mybir.AxisListType
+
+P = 128
+ROWS = 16
+CH = ROWS * W
+NCHUNK = H // ROWS
+NSTEP = NH * NCHUNK
+TRI = 3 * W
+NATW = (ROWS // 2) * TRI + W
+MOVW = H * W + W
+XV = 512
+NB = 2
+NEG = -1.0e9
+Y_SCALE = 12000.0
+
+
+def tile_multiheadcrisscrossattention_pa_kernel(tc, q, k, out_0, out_1):
+    nc = tc.nc
+    qv = q.rearrange("b n (p t) h w -> (b n) p t (h w)", t=4)
+    kv = k.rearrange("b n (p t) h w -> (b n) p t (h w)", t=4)
+    o0v = out_0.rearrange("b n h w j -> (b n) (h w) j").rearrange("n (s p) j -> n p s j", p=P)
+    o1v = out_1.rearrange("b n h w j -> (b n) (h w) j").rearrange("n (s p) j -> n p s j", p=P)
+
+    with ExitStack() as ctx:
+        const = ctx.enter_context(tc.tile_pool(name="const", bufs=1))
+        keep = ctx.enter_context(tc.tile_pool(name="keep", bufs=1))
+        rawp = ctx.enter_context(tc.tile_pool(name="rawp", bufs=4))
+        gp = ctx.enter_context(tc.tile_pool(name="gp", bufs=4))
+        pp = ctx.enter_context(tc.tile_pool(name="pp", bufs=2))
+        f8p = ctx.enter_context(tc.tile_pool(name="f8p", bufs=2))
+        stat = ctx.enter_context(tc.tile_pool(name="stat", bufs=2))
+        psw = ctx.enter_context(tc.psum_pool(name="psw", bufs=2))
+        psh = ctx.enter_context(tc.psum_pool(name="psh", bufs=3))
+        pst = ctx.enter_context(tc.psum_pool(name="pst", bufs=3))
+
+        w2 = const.tile([P, 2 * P], F32, name="w2")
+        make_identity(nc, w2[:, 0:P])
+        make_identity(nc, w2[:, P : 2 * P])
+        cmask = const.tile([P, P], F32, name="cmask")
+        nc.vector.tensor_scalar(out=cmask[:, 0:W], in0=w2[:, 0:1].to_broadcast([P, W]), scalar1=NEG, scalar2=None, op0=ALU.mult)
+        nc.vector.tensor_scalar(out=cmask[:, W:P], in0=w2[:, 1:2].to_broadcast([P, W]), scalar1=NEG, scalar2=None, op0=ALU.mult)
+        warm_in = const.tile([P, 1], F32, name="warm_in")
+        warm_out = const.tile([P, 1], F32, name="warm_out")
+        nc.vector.memset(warm_in[:], 0.0)
+        nc.scalar.activation(out=warm_out[:], in_=warm_in[:], func=ACT.Exp)
+
+        natq, natk, nats = [], [], []
+        for b in range(NB):
+            tq = keep.tile([P, NATW], I32, name="natq%d" % b, align_bytes=64)
+            tk = keep.tile([P, NATW], I32, name="natk%d" % b, align_bytes=64)
+            ts = keep.tile([P, NATW], U8, name="nats%d" % b, align_bytes=64)
+            nc.vector.memset(tq[:], 0)
+            nc.vector.memset(tk[:], 0)
+            nc.vector.memset(ts[:].bitcast(I32), 0)
+            natq.append(tq)
+            natk.append(tk)
+            nats.append(ts)
+        movq, movk, movs = [], [], []
+        for b in range(2):
+            tq = keep.tile([P, MOVW], I32, name="movq%d" % b, align_bytes=64)
+            tk = keep.tile([P, MOVW], I32, name="movk%d" % b, align_bytes=64)
+            ts = keep.tile([P, MOVW], U8, name="movs%d" % b, align_bytes=64)
+            nc.vector.memset(tq[:, H * W : MOVW], 0)
+            nc.vector.memset(tk[:, H * W : MOVW], 0)
+            nc.vector.memset(ts[:, H * W : MOVW].bitcast(I32), 0)
+            movq.append(tq)
+            movk.append(tk)
+            movs.append(ts)
+        s2 = keep.tile([P, H * W], F32, name="s2")
+        s2v = s2[:].rearrange("p (h w) -> p h w", w=W)
+
+        raws = {}
+        gs = {}
+        head = {}
+
+        def load(t):
+            n, c = divmod(t, NCHUNK)
+            for nm, src in (("q", qv), ("k", kv)):
+                r = rawp.tile([P, 4, CH], BF16, name="raw", tag="raw")
+                nc.sync.dma_start(out=r[:], in_=src[n, :, :, c * CH : (c + 1) * CH])
+                raws[(t, nm)] = r
+
+        def interleave(t):
+            for nm in ("q", "k"):
+                r = raws[(t, nm)]
+                g = gp.tile([P, 4 * CH], BF16, name="g", tag="g", align_bytes=64)
+                gv = g[:].rearrange("p (c t) -> p c t", t=4)
+                rv = r[:].rearrange("p t c -> p c t")
+                nc.vector.tensor_copy(out=gv[:, 0:XV, :], in_=rv[:, 0:XV, :])
+                nc.scalar.copy(out=gv[:, XV:CH, :], in_=rv[:, XV:CH, :])
+                gs[(t, nm)] = g
+
+        def quantise(t):
+            b = t % NB
+            rw = 4 * W
+            gq = gs[(t, "q")]
+            gk = gs[(t, "k")]
+            calls = [(0, 1, 0)]
+            calls.extend([(2 * u + 1, 2, TRI * u + 2 * W) for u in range(ROWS // 2 - 1)])
+            calls.append((ROWS - 1, 1, TRI * (ROWS // 2 - 1) + 2 * W))
+            for r0, nr, pos in calls:
+                nc.vector.quantize_mx(
+                    out=natq[b][:, pos : pos + nr * W].bitcast(FP8X4),
+                    scales=nats[b][:, pos : pos + nr * W],
+                    in_=gq[:, r0 * rw : (r0 + nr) * rw],
+                )
+            calls = [(0, 2, 0)]
+            calls.extend([(2 * u + 1, 2, TRI * u + 2 * W) for u in range(ROWS // 2 - 1)])
+            calls.append((ROWS - 2, 2, TRI * (ROWS // 2 - 1) + W))
+            for r0, nr, pos in calls:
+                nc.vector.quantize_mx(
+                    out=natk[b][:, pos : pos + nr * W].bitcast(FP8X4),
+                    scales=nats[b][4:P, pos : pos + nr * W],
+                    in_=gk[:, r0 * rw : (r0 + nr) * rw],
+                )
+
+        def new_head(n):
+            d = {}
+            d["p"] = pp.tile([P, H // 2, P], F32, name="prob", tag="prob")
+            for nm in ("nmw", "sw", "nm", "sh"):
+                d[nm] = stat.tile([P, H // 2], F32, name=nm, tag=nm)
+            d["f"] = stat.tile([P, H // 2, 2], F32, name="fac", tag="fac")
+            head[n] = d
+
+        def row_energies(t):
+            n, c = divmod(t, NCHUNK)
+            if c == 0:
+                new_head(n)
+            d = head[n]
+            b = t % NB
+            banks = []
+            for u in range(ROWS // 2):
+                if u % 4 == 0:
+                    ew = psw.tile([P, 4, P], F32, name="ew", tag="ew")
+                    banks.append(ew)
+                a = TRI * u
+                nc.tensor.matmul_mx(
+                    out=ew[:, u % 4, :],
+                    lhsT=natq[b][:, a : a + P].bitcast(FP8X4),
+                    lhsT_scale=nats[b][:, a : a + P],
+                    rhs=natk[b][:, a : a + P].bitcast(FP8X4),
+                    rhs_scale=nats[b][4:P, a : a + P],
+                    start=True,
+                    stop=False,
+                )
+                nc.tensor.matmul_mx(
+                    out=ew[:, u % 4, :],
+                    lhsT=natq[b][:, a + W : a + W + P].bitcast(FP8X4),
+                    lhsT_scale=nats[b][:, a + W : a + W + P],
+                    rhs=natk[b][:, a + 2 * W : a + 2 * W + P].bitcast(FP8X4),
+                    rhs_scale=nats[b][4:P, a + 2 * W : a + 2 * W + P],
+                    start=False,
+                    stop=True,
+                )
+            d["ew%d" % c] = banks
+
+        def moves(t):
+            n, c = divmod(t, NCHUNK)
+            b = t % NB
+            m = n % 2
+            h0 = c * ROWS
+            for src, dst in ((natq[b], movq[m]), (natk[b], movk[m]), (nats[b], movs[m])):
+                sv = src[:, 0 : NATW - W].rearrange("p (g u x w) -> p g u x w", g=4, u=2, x=3)[:, :, :, 0:3:2, :]
+                dv = dst[:, 0 : H * W].rearrange("p (w h) -> p w h", h=H)[:, :, h0 : h0 + ROWS]
+                nc.vector.tensor_copy(
+                    out=dv.rearrange("p w (g u v) -> p g w u v", g=4, u=2),
+                    in_=sv.rearrange("p g u v w -> p g w u v"),
+                )
+
+        def row_softmax(t):
+            n, c = divmod(t, NCHUNK)
+            d = head[n]
+            banks = d["ew%d" % c]
+            s0 = c * (ROWS // 2)
+            mwt = stat.tile([P, ROWS // 2], F32, name="mwt", tag="mwt")
+            for i, ew in enumerate(banks):
+                nc.vector.tensor_reduce(out=mwt[:, 4 * i : 4 * i + 4], in_=ew[:, :, 0:W], axis=AX.X, op=ALU.max)
+            nc.vector.tensor_scalar(out=d["nmw"][:, s0 : s0 + ROWS // 2], in0=mwt[:], scalar1=-1.0, scalar2=None, op0=ALU.mult)
+            for u in range(ROWS // 2):
+                s = s0 + u
+                nc.scalar.activation(
+                    out=d["p"][:, s, W:P],
+                    in_=banks[u // 4][:, u % 4, 0:W],
+                    func=ACT.Exp,
+                    bias=d["nmw"][:, s : s + 1],
+                    scale=1.0,
+                    accum_out=d["sw"][:, s : s + 1],
+                )
+
+        def col_energies(n):
+            m = n % 2
+            for wq in range(W // 4):
+                eh = psh.tile([P, 4, P], F32, name="eh", tag="eh")
+                for i in range(4):
+                    a = (4 * wq + i) * H
+                    nc.tensor.matmul_mx(
+                        out=eh[:, i, :],
+                        lhsT=movk[m][:, a : a + P].bitcast(FP8X4),
+                        lhsT_scale=movs[m][4:P, a : a + P],
+                        rhs=movq[m][:, a : a + P].bitcast(FP8X4),
+                        rhs_scale=movs[m][:, a : a + P],
+                        start=True,
+                        stop=True,
+                    )
+                nc.scalar.copy(out=s2v[:, :, 4 * wq : 4 * wq + 4], in_=eh[:, :, 0:H].rearrange("p w h -> p h w"))
+
+        def col_softmax(n, banks):
+            d = head[n]
+            for sq in banks:
+                et = pst.tile([P, 4, P], F32, name="et", tag="et")
+                for i in range(4):
+                    s = 4 * sq + i
+                    nc.tensor.matmul(out=et[:, i, :], lhsT=s2[:, P * s : P * (s + 1)], rhs=w2[:, 0:P], is_transpose=True, start=True, stop=False)
+                    nc.tensor.matmul(out=et[:, i, :], lhsT=cmask[:], rhs=w2[:, P - 2 * s : 2 * P - 2 * s], is_transpose=True, start=False, stop=True)
+                mht = stat.tile([P, 4], F32, name="mht", tag="mht")
+                nc.vector.tensor_reduce(out=mht[:], in_=et[:, :, 0:H], axis=AX.X, op=ALU.max)
+                nc.vector.scalar_tensor_tensor(
+                    out=d["nm"][:, 4 * sq : 4 * sq + 4], in0=mht[:], scalar=-1.0, in1=d["nmw"][:, 4 * sq : 4 * sq + 4], op0=ALU.mult, op1=ALU.min
+                )
+                for i in range(4):
+                    s = 4 * sq + i
+                    nc.scalar.activation(
+                        out=d["p"][:, s, 0:H],
+                        in_=et[:, i, 0:H],
+                        func=ACT.Exp,
+                        bias=d["nm"][:, s : s + 1],
+                        scale=1.0,
+                        accum_out=d["sh"][:, s : s + 1],
+                    )
+
+        def factors(n, g):
+            d = head[n]
+            sl = slice(16 * g, 16 * g + 16)
+            dw = stat.tile([P, 16], F32, name="dw", tag="dw")
+            ef = stat.tile([P, 16], F32, name="ef", tag="ef")
+            tot = stat.tile([P, 16], F32, name="tot", tag="tot")
+            nc.vector.tensor_tensor(out=dw[:], in0=d["nm"][:, sl], in1=d["nmw"][:, sl], op=ALU.subtract)
+            nc.scalar.activation(out=ef[:], in_=dw[:], func=ACT.Exp)
+            nc.vector.tensor_tensor(out=tot[:], in0=d["sw"][:, sl], in1=ef[:], op=ALU.mult)
+            nc.vector.tensor_tensor(out=tot[:], in0=tot[:], in1=d["sh"][:, sl], op=ALU.add)
+            nc.vector.reciprocal(out=d["f"][:, sl, 0], in_=tot[:])
+            nc.vector.tensor_tensor(out=d["f"][:, sl, 1], in0=ef[:], in1=d["f"][:, sl, 0], op=ALU.mult)
+
+        def finish(n, g):
+            d = head[n]
+            pr = d["p"]
+            for s in range(16 * g, 16 * g + 16):
+                for hf in range(2):
+                    nc.scalar.activation(
+                        out=pr[:, s, hf * W : (hf + 1) * W],
+                        in_=pr[:, s, hf * W : (hf + 1) * W],
+                        func=ACT.Copy,
+                        scale=d["f"][:, s, hf : hf + 1],
+                    )
+            nc.sync.dma_start(out=o0v[n, :, 16 * g : 16 * g + 16, :], in_=pr[:, 16 * g : 16 * g + 16, :])
+            f8 = f8p.tile([P, 16, P], FP8, name="f8", tag="f8")
+            nc.vector.tensor_scalar(out=f8[:], in0=pr[:, 16 * g : 16 * g + 16, :], scalar1=Y_SCALE, scalar2=None, op0=ALU.mult, saturate=False)
+            for i in range(4):
+                s = 16 * g + 4 * i
+                nc.sync.dma_start(out=o1v[n, :, s : s + 4, :], in_=f8[:, 4 * i : 4 * i + 4, :].bitcast(U8))
+
+        load(0)
+        load(1)
+        interleave(0)
+        for t in range(NSTEP + NCHUNK):
+            if t + 2 < NSTEP:
+                load(t + 2)
+            if t + 1 < NSTEP:
+                interleave(t + 1)
+            if t < NSTEP:
+                quantise(t)
+                row_energies(t)
+            n, e = divmod(t - NCHUNK, NCHUNK)
+            if n >= 0:
+                if e == 0:
+                    col_energies(n)
+                elif e == 1:
+                    col_softmax(n, range(0, 4))
+                    factors(n, 0)
+                elif e == 2:
+                    finish(n, 0)
+                    col_softmax(n, range(4, 8))
+                    factors(n, 1)
+                else:
+                    finish(n, 1)
+            if t < NSTEP:
+                moves(t)
+                row_softmax(t)

@@ -24,7 +24,8 @@ NSTEP = NH * NCHUNK
 TRI = 3 * W
 NATW = (ROWS // 2) * TRI + W
 MOVW = H * W + W
-XV = 512
+XV = 432
+XV0 = 768
 NB = 2
 NEG = -1.0e9
 Y_SCALE = 12000.0
@@ -45,9 +46,7 @@ def tile_multiheadcrisscrossattention_pa_kernel(tc, q, k, out_0, out_1):
         pp = ctx.enter_context(tc.tile_pool(name="pp", bufs=2))
         f8p = ctx.enter_context(tc.tile_pool(name="f8p", bufs=2))
         stat = ctx.enter_context(tc.tile_pool(name="stat", bufs=2))
-        psw = ctx.enter_context(tc.psum_pool(name="psw", bufs=2))
-        psh = ctx.enter_context(tc.psum_pool(name="psh", bufs=3))
-        pst = ctx.enter_context(tc.psum_pool(name="pst", bufs=3))
+        psum = ctx.enter_context(tc.psum_pool(name="psum", bufs=8))
 
         w2 = const.tile([P, 2 * P], F32, name="w2")
         make_identity(nc, w2[:, 0:P])
@@ -65,9 +64,9 @@ def tile_multiheadcrisscrossattention_pa_kernel(tc, q, k, out_0, out_1):
             tq = keep.tile([P, NATW], I32, name="natq%d" % b, align_bytes=64)
             tk = keep.tile([P, NATW], I32, name="natk%d" % b, align_bytes=64)
             ts = keep.tile([P, NATW], U8, name="nats%d" % b, align_bytes=64)
-            nc.vector.memset(tq[:], 0)
-            nc.vector.memset(tk[:], 0)
-            nc.vector.memset(ts[:].bitcast(I32), 0)
+            for view, gw in ((tq[:], W), (tk[:], W), (ts[:].bitcast(I32), W // 4)):
+                nc.vector.memset(view[:, 0 : 24 * gw].rearrange("p (u x w) -> p u x w", x=3, w=gw)[:, :, 1, :], 0)
+                nc.vector.memset(view[:, 24 * gw : 25 * gw], 0)
             natq.append(tq)
             natk.append(tk)
             nats.append(ts)
@@ -91,20 +90,28 @@ def tile_multiheadcrisscrossattention_pa_kernel(tc, q, k, out_0, out_1):
 
         def load(t):
             n, c = divmod(t, NCHUNK)
-            for nm, src in (("q", qv), ("k", kv)):
-                r = rawp.tile([P, 4, CH], BF16, name="raw", tag="raw")
-                nc.sync.dma_start(out=r[:], in_=src[n, :, :, c * CH : (c + 1) * CH])
-                raws[(t, nm)] = r
+            for nm in ("q", "k"):
+                raws[(t, nm)] = rawp.tile([P, 4, CH], BF16, name="raw", tag="raw")
+            pieces = (0, 3, 1, 2) if t == 0 else (0,)
+            pw = CH // len(pieces)
+            for i in pieces:
+                for nm, src in (("q", qv), ("k", kv)):
+                    nc.sync.dma_start(out=raws[(t, nm)][:, :, i * pw : (i + 1) * pw], in_=src[n, :, :, c * CH + i * pw : c * CH + (i + 1) * pw])
 
         def interleave(t):
+            xv = XV0 if t == 0 else XV
+            step = 256 if t == 0 else CH
             for nm in ("q", "k"):
-                r = raws[(t, nm)]
-                g = gp.tile([P, 4 * CH], BF16, name="g", tag="g", align_bytes=64)
-                gv = g[:].rearrange("p (c t) -> p c t", t=4)
-                rv = r[:].rearrange("p t c -> p c t")
-                nc.vector.tensor_copy(out=gv[:, 0:XV, :], in_=rv[:, 0:XV, :])
-                nc.scalar.copy(out=gv[:, XV:CH, :], in_=rv[:, XV:CH, :])
-                gs[(t, nm)] = g
+                gs[(t, nm)] = gp.tile([P, 4 * CH], BF16, name="g", tag="g", align_bytes=64)
+            for a in range(0, CH, step):
+                for nm in ("q", "k"):
+                    gv = gs[(t, nm)][:].rearrange("p (c t) -> p c t", t=4)
+                    rv = raws[(t, nm)][:].rearrange("p t c -> p c t")
+                    b = min(a + step, CH)
+                    if a < xv:
+                        nc.vector.tensor_copy(out=gv[:, a : min(b, xv), :], in_=rv[:, a : min(b, xv), :])
+                    if b > xv:
+                        nc.scalar.copy(out=gv[:, max(a, xv) : b, :], in_=rv[:, max(a, xv) : b, :])
 
         def quantise(t):
             b = t % NB
@@ -147,7 +154,7 @@ def tile_multiheadcrisscrossattention_pa_kernel(tc, q, k, out_0, out_1):
             banks = []
             for u in range(ROWS // 2):
                 if u % 4 == 0:
-                    ew = psw.tile([P, 4, P], F32, name="ew", tag="ew")
+                    ew = psum.tile([P, 4, P], F32, name="ew", tag="bank")
                     banks.append(ew)
                 a = TRI * u
                 nc.tensor.matmul_mx(
@@ -206,7 +213,7 @@ def tile_multiheadcrisscrossattention_pa_kernel(tc, q, k, out_0, out_1):
         def col_energies(n):
             m = n % 2
             for wq in range(W // 4):
-                eh = psh.tile([P, 4, P], F32, name="eh", tag="eh")
+                eh = psum.tile([P, 4, P], F32, name="eh", tag="bank")
                 for i in range(4):
                     a = (4 * wq + i) * H
                     nc.tensor.matmul_mx(
@@ -223,7 +230,7 @@ def tile_multiheadcrisscrossattention_pa_kernel(tc, q, k, out_0, out_1):
         def col_softmax(n, banks):
             d = head[n]
             for sq in banks:
-                et = pst.tile([P, 4, P], F32, name="et", tag="et")
+                et = psum.tile([P, 4, P], F32, name="et", tag="bank")
                 for i in range(4):
                     s = 4 * sq + i
                     nc.tensor.matmul(out=et[:, i, :], lhsT=s2[:, P * s : P * (s + 1)], rhs=w2[:, 0:P], is_transpose=True, start=True, stop=False)
@@ -244,61 +251,74 @@ def tile_multiheadcrisscrossattention_pa_kernel(tc, q, k, out_0, out_1):
                         accum_out=d["sh"][:, s : s + 1],
                     )
 
-        def factors(n, g):
+        def factors(n, s0, ns):
             d = head[n]
-            sl = slice(16 * g, 16 * g + 16)
+            sl = slice(s0, s0 + ns)
             dw = stat.tile([P, 16], F32, name="dw", tag="dw")
             ef = stat.tile([P, 16], F32, name="ef", tag="ef")
             tot = stat.tile([P, 16], F32, name="tot", tag="tot")
-            nc.vector.tensor_tensor(out=dw[:], in0=d["nm"][:, sl], in1=d["nmw"][:, sl], op=ALU.subtract)
-            nc.scalar.activation(out=ef[:], in_=dw[:], func=ACT.Exp)
-            nc.vector.tensor_tensor(out=tot[:], in0=d["sw"][:, sl], in1=ef[:], op=ALU.mult)
-            nc.vector.tensor_tensor(out=tot[:], in0=tot[:], in1=d["sh"][:, sl], op=ALU.add)
-            nc.vector.reciprocal(out=d["f"][:, sl, 0], in_=tot[:])
-            nc.vector.tensor_tensor(out=d["f"][:, sl, 1], in0=ef[:], in1=d["f"][:, sl, 0], op=ALU.mult)
+            nc.vector.tensor_tensor(out=dw[:, 0:ns], in0=d["nm"][:, sl], in1=d["nmw"][:, sl], op=ALU.subtract)
+            nc.scalar.activation(out=ef[:, 0:ns], in_=dw[:, 0:ns], func=ACT.Exp)
+            nc.vector.tensor_tensor(out=tot[:, 0:ns], in0=d["sw"][:, sl], in1=ef[:, 0:ns], op=ALU.mult)
+            nc.vector.tensor_tensor(out=tot[:, 0:ns], in0=tot[:, 0:ns], in1=d["sh"][:, sl], op=ALU.add)
+            nc.vector.reciprocal(out=d["f"][:, sl, 0], in_=tot[:, 0:ns])
+            nc.vector.tensor_tensor(out=d["f"][:, sl, 1], in0=ef[:, 0:ns], in1=d["f"][:, sl, 0], op=ALU.mult)
 
-        def finish(n, g):
+        def finish(n, s0, ns, on_vector):
             d = head[n]
             pr = d["p"]
-            for s in range(16 * g, 16 * g + 16):
-                for hf in range(2):
-                    nc.scalar.activation(
-                        out=pr[:, s, hf * W : (hf + 1) * W],
-                        in_=pr[:, s, hf * W : (hf + 1) * W],
-                        func=ACT.Copy,
-                        scale=d["f"][:, s, hf : hf + 1],
-                    )
-            nc.sync.dma_start(out=o0v[n, :, 16 * g : 16 * g + 16, :], in_=pr[:, 16 * g : 16 * g + 16, :])
+            sl = slice(s0, s0 + ns)
+            if on_vector:
+                pv = pr[:, sl, :].rearrange("p s (f j) -> p (s f) j", f=2)
+                fv = d["f"][:, sl, :].rearrange("p s f -> p (s f)").unsqueeze(2).to_broadcast([P, 2 * ns, W])
+                nc.vector.tensor_tensor(out=pv, in0=pv, in1=fv, op=ALU.mult)
+            else:
+                for s in range(s0, s0 + ns):
+                    for hf in range(2):
+                        nc.scalar.activation(
+                            out=pr[:, s, hf * W : (hf + 1) * W],
+                            in_=pr[:, s, hf * W : (hf + 1) * W],
+                            func=ACT.Copy,
+                            scale=d["f"][:, s, hf : hf + 1],
+                        )
+            nc.sync.dma_start(out=o0v[n, :, sl, :], in_=pr[:, sl, :])
             f8 = f8p.tile([P, 16, P], FP8, name="f8", tag="f8")
-            nc.vector.tensor_scalar(out=f8[:], in0=pr[:, 16 * g : 16 * g + 16, :], scalar1=Y_SCALE, scalar2=None, op0=ALU.mult, saturate=False)
-            for i in range(4):
-                s = 16 * g + 4 * i
+            nc.vector.tensor_scalar(out=f8[:, 0:ns, :], in0=pr[:, sl, :], scalar1=Y_SCALE, scalar2=None, op0=ALU.mult, saturate=False)
+            for i in range(ns // 4):
+                s = s0 + 4 * i
                 nc.sync.dma_start(out=o1v[n, :, s : s + 4, :], in_=f8[:, 4 * i : 4 * i + 4, :].bitcast(U8))
 
         load(0)
         load(1)
         interleave(0)
-        for t in range(NSTEP + NCHUNK):
+        for t in range(NSTEP):
             if t + 2 < NSTEP:
                 load(t + 2)
             if t + 1 < NSTEP:
                 interleave(t + 1)
-            if t < NSTEP:
-                quantise(t)
-                row_energies(t)
+            quantise(t)
+            row_energies(t)
+            moves(t)
+            row_softmax(t)
             n, e = divmod(t - NCHUNK, NCHUNK)
             if n >= 0:
                 if e == 0:
                     col_energies(n)
                 elif e == 1:
                     col_softmax(n, range(0, 4))
-                    factors(n, 0)
+                    factors(n, 0, 16)
                 elif e == 2:
-                    finish(n, 0)
+                    if n == 0:
+                        finish(n, 0, 16, False)
                     col_softmax(n, range(4, 8))
-                    factors(n, 1)
-                else:
-                    finish(n, 1)
-            if t < NSTEP:
-                moves(t)
-                row_softmax(t)
+                    factors(n, 16, 16)
+                elif n == 0:
+                    finish(n, 16, 16, False)
+        n = NH - 1
+        col_energies(n)
+        for g in range(4):
+            col_softmax(n, range(2 * g, 2 * g + 2))
+            factors(n, 8 * g, 8)
+            finish(n, 8 * g, 8, True)
+        finish(n - 1, 0, 16, False)
+        finish(n - 1, 16, 16, False)

@@ -105,13 +105,13 @@ def tile_multiheadcrisscrossattention_pa_kernel(tc, q, k, out_0, out_1):
                 gs[(t, nm)] = gp.tile([P, 4 * CH], BF16, name="g", tag="g", align_bytes=64)
             for a in range(0, CH, step):
                 for nm in ("q", "k"):
-                    gv = gs[(t, nm)][:].rearrange("p (c t) -> p c t", t=4)
-                    rv = raws[(t, nm)][:].rearrange("p t c -> p c t")
+                    gv = gs[(t, nm)][:].rearrange("p (c i t) -> p c t i", i=4, t=4)
+                    rv = raws[(t, nm)][:].rearrange("p t (c i) -> p c t i", i=4)
                     b = min(a + step, CH)
                     if a < xv:
-                        nc.vector.tensor_copy(out=gv[:, a : min(b, xv), :], in_=rv[:, a : min(b, xv), :])
+                        nc.vector.tensor_copy(out=gv[:, a // 4 : min(b, xv) // 4, :, :], in_=rv[:, a // 4 : min(b, xv) // 4, :, :])
                     if b > xv:
-                        nc.scalar.copy(out=gv[:, max(a, xv) : b, :], in_=rv[:, max(a, xv) : b, :])
+                        nc.scalar.copy(out=gv[:, max(a, xv) // 4 : b // 4, :, :], in_=rv[:, max(a, xv) // 4 : b // 4, :, :])
 
         def quantise(t):
             b = t % NB
@@ -182,13 +182,15 @@ def tile_multiheadcrisscrossattention_pa_kernel(tc, q, k, out_0, out_1):
             b = t % NB
             m = n % 2
             h0 = c * ROWS
-            for src, dst in ((natq[b], movq[m]), (natk[b], movk[m]), (nats[b], movs[m])):
-                sv = src[:, 0 : NATW - W].rearrange("p (g u x w) -> p g u x w", g=4, u=2, x=3)[:, :, :, 0:3:2, :]
-                dv = dst[:, 0 : H * W].rearrange("p (w h) -> p w h", h=H)[:, :, h0 : h0 + ROWS]
-                nc.vector.tensor_copy(
-                    out=dv.rearrange("p w (g u v) -> p g w u v", g=4, u=2),
-                    in_=sv.rearrange("p g u v w -> p g w u v"),
-                )
+            wstep = W // 4 if t == NSTEP - 1 else W
+            for w0 in range(0, W, wstep):
+                for src, dst in ((natq[b], movq[m]), (natk[b], movk[m]), (nats[b], movs[m])):
+                    sv = src[:, 0 : NATW - W].rearrange("p (g u x w) -> p g u x w", g=4, u=2, x=3)[:, :, :, 0:3:2, w0 : w0 + wstep]
+                    dv = dst[:, 0 : H * W].rearrange("p (w h) -> p w h", h=H)[:, w0 : w0 + wstep, h0 : h0 + ROWS]
+                    nc.vector.tensor_copy(
+                        out=dv.rearrange("p w (g u v) -> p g w u v", g=4, u=2),
+                        in_=sv.rearrange("p g u v w -> p g w u v"),
+                    )
 
         def row_softmax(t):
             n, c = divmod(t, NCHUNK)
@@ -225,7 +227,10 @@ def tile_multiheadcrisscrossattention_pa_kernel(tc, q, k, out_0, out_1):
                         start=True,
                         stop=True,
                     )
-                nc.scalar.copy(out=s2v[:, :, 4 * wq : 4 * wq + 4], in_=eh[:, :, 0:H].rearrange("p w h -> p h w"))
+                if n == NH - 1 and wq % 2 == 1:
+                    nc.vector.tensor_copy(out=s2v[:, :, 4 * wq : 4 * wq + 4], in_=eh[:, :, 0:H].rearrange("p w h -> p h w"))
+                else:
+                    nc.scalar.copy(out=s2v[:, :, 4 * wq : 4 * wq + 4], in_=eh[:, :, 0:H].rearrange("p w h -> p h w"))
 
         def col_softmax(n, banks):
             d = head[n]
@@ -308,17 +313,15 @@ def tile_multiheadcrisscrossattention_pa_kernel(tc, q, k, out_0, out_1):
                     col_softmax(n, range(0, 4))
                     factors(n, 0, 16)
                 elif e == 2:
-                    if n == 0:
-                        finish(n, 0, 16, False)
+                    finish(n, 0, 16, False)
                     col_softmax(n, range(4, 8))
                     factors(n, 16, 16)
                 elif n == 0:
                     finish(n, 16, 16, False)
         n = NH - 1
         col_energies(n)
+        finish(n - 1, 16, 16, False)
         for g in range(4):
             col_softmax(n, range(2 * g, 2 * g + 2))
             factors(n, 8 * g, 8)
-            finish(n, 8 * g, 8, True)
-        finish(n - 1, 0, 16, False)
-        finish(n - 1, 16, 16, False)
+            finish(n, 8 * g, 8, False)

@@ -22,11 +22,14 @@ CH = ROWS * W
 NCHUNK = H // ROWS
 NSTEP = NH * NCHUNK
 TRI = 3 * W
-NATW = (ROWS // 2) * TRI + W
+NATW = W + (ROWS // 2) * TRI
+NATKW = W + CH
 MOVW = H * W + W
 XV = 432
 XV0 = 768
-NB = 2
+XV1 = 304
+RING = 6
+AHEAD = 4
 NEG = -1.0e9
 Y_SCALE = 12000.0
 
@@ -43,9 +46,9 @@ def tile_multiheadcrisscrossattention_pa_kernel(tc, q, k, out_0, out_1):
         keep = ctx.enter_context(tc.tile_pool(name="keep", bufs=1))
         rawp = ctx.enter_context(tc.tile_pool(name="rawp", bufs=4))
         gp = ctx.enter_context(tc.tile_pool(name="gp", bufs=4))
-        pp = ctx.enter_context(tc.tile_pool(name="pp", bufs=2))
-        f8p = ctx.enter_context(tc.tile_pool(name="f8p", bufs=2))
-        stat = ctx.enter_context(tc.tile_pool(name="stat", bufs=2))
+        pp = ctx.enter_context(tc.tile_pool(name="pp", bufs=9))
+        f8p = ctx.enter_context(tc.tile_pool(name="f8p", bufs=3))
+        stat = ctx.enter_context(tc.tile_pool(name="stat", bufs=4))
         psum = ctx.enter_context(tc.psum_pool(name="psum", bufs=8))
 
         w2 = const.tile([P, 2 * P], F32, name="w2")
@@ -54,39 +57,46 @@ def tile_multiheadcrisscrossattention_pa_kernel(tc, q, k, out_0, out_1):
         cmask = const.tile([P, P], F32, name="cmask")
         nc.vector.tensor_scalar(out=cmask[:, 0:W], in0=w2[:, 0:1].to_broadcast([P, W]), scalar1=NEG, scalar2=None, op0=ALU.mult)
         nc.vector.tensor_scalar(out=cmask[:, W:P], in0=w2[:, 1:2].to_broadcast([P, W]), scalar1=NEG, scalar2=None, op0=ALU.mult)
+        maskj = const.tile([P, H], F32, name="maskj")
+        nc.vector.tensor_scalar(out=maskj[:], in0=w2[:, 0:H], scalar1=NEG, scalar2=None, op0=ALU.mult)
         warm_in = const.tile([P, 1], F32, name="warm_in")
         warm_out = const.tile([P, 1], F32, name="warm_out")
         nc.vector.memset(warm_in[:], 0.0)
         nc.scalar.activation(out=warm_out[:], in_=warm_in[:], func=ACT.Exp)
 
         natq, natk, nats = [], [], []
-        for b in range(NB):
+        for b in range(RING):
             tq = keep.tile([P, NATW], I32, name="natq%d" % b, align_bytes=64)
-            tk = keep.tile([P, NATW], I32, name="natk%d" % b, align_bytes=64)
+            tk = keep.tile([P, NATKW], I32, name="natk%d" % b, align_bytes=64)
             ts = keep.tile([P, NATW], U8, name="nats%d" % b, align_bytes=64)
-            for view, gw in ((tq[:], W), (tk[:], W), (ts[:].bitcast(I32), W // 4)):
-                nc.vector.memset(view[:, 0 : 24 * gw].rearrange("p (u x w) -> p u x w", x=3, w=gw)[:, :, 1, :], 0)
-                nc.vector.memset(view[:, 24 * gw : 25 * gw], 0)
             natq.append(tq)
             natk.append(tk)
             nats.append(ts)
-        movq, movk, movs = [], [], []
-        for b in range(2):
-            tq = keep.tile([P, MOVW], I32, name="movq%d" % b, align_bytes=64)
-            tk = keep.tile([P, MOVW], I32, name="movk%d" % b, align_bytes=64)
-            ts = keep.tile([P, MOVW], U8, name="movs%d" % b, align_bytes=64)
-            nc.vector.memset(tq[:, H * W : MOVW], 0)
-            nc.vector.memset(tk[:, H * W : MOVW], 0)
-            nc.vector.memset(ts[:, H * W : MOVW].bitcast(I32), 0)
-            movq.append(tq)
-            movk.append(tk)
-            movs.append(ts)
+
+        def init_ring(b):
+            sv = nats[b][:].bitcast(I32)
+            nc.vector.memset(natq[b][:, W:NATW].rearrange("p (u x w) -> p u x w", x=3, w=W)[:, :, 1, :], 0)
+            nc.vector.memset(sv[:, W // 4 : NATW // 4].rearrange("p (u x w) -> p u x w", x=3, w=W // 4)[:, :, 1, :], 0)
+            nc.vector.memset(sv[:, 0 : W // 4], 0)
+            nc.vector.memset(natk[b][:, 0:W], 0)
+
+        init_ring(0)
+        init_ring(1)
+        movq = keep.tile([P, MOVW], I32, name="movq", align_bytes=64)
+        movk = keep.tile([P, MOVW], I32, name="movk", align_bytes=64)
+        movs = keep.tile([P, MOVW], U8, name="movs", align_bytes=64)
+        nc.vector.memset(movq[:, H * W : MOVW], 0)
+        nc.vector.memset(movk[:, H * W : MOVW], 0)
+        nc.vector.memset(movs[:, H * W : MOVW].bitcast(I32), 0)
         s2 = keep.tile([P, H * W], F32, name="s2")
         s2v = s2[:].rearrange("p (h w) -> p h w", w=W)
 
         raws = {}
         gs = {}
-        head = {}
+        prob = {}
+        banks = {}
+        sums = {}
+        recs = {}
 
         def load(t):
             n, c = divmod(t, NCHUNK)
@@ -99,7 +109,7 @@ def tile_multiheadcrisscrossattention_pa_kernel(tc, q, k, out_0, out_1):
                     nc.sync.dma_start(out=raws[(t, nm)][:, :, i * pw : (i + 1) * pw], in_=src[n, :, :, c * CH + i * pw : c * CH + (i + 1) * pw])
 
         def interleave(t):
-            xv = XV0 if t == 0 else XV
+            xv = XV0 if t == 0 else (XV1 if t <= NCHUNK else XV)
             step = 256 if t == 0 else CH
             for nm in ("q", "k"):
                 gs[(t, nm)] = gp.tile([P, 4 * CH], BF16, name="g", tag="g", align_bytes=64)
@@ -114,214 +124,184 @@ def tile_multiheadcrisscrossattention_pa_kernel(tc, q, k, out_0, out_1):
                         nc.scalar.copy(out=gv[:, max(a, xv) // 4 : b // 4, :, :], in_=rv[:, max(a, xv) // 4 : b // 4, :, :])
 
         def quantise(t):
-            b = t % NB
+            b = t % RING
             rw = 4 * W
             gq = gs[(t, "q")]
             gk = gs[(t, "k")]
-            calls = [(0, 1, 0)]
-            calls.extend([(2 * u + 1, 2, TRI * u + 2 * W) for u in range(ROWS // 2 - 1)])
-            calls.append((ROWS - 1, 1, TRI * (ROWS // 2 - 1) + 2 * W))
-            for r0, nr, pos in calls:
+            mid = [(2 * u + 1, 2, W + TRI * u + 2 * W) for u in range(ROWS // 2 - 1)]
+            for r0, nr, pos in [(0, 1, W)] + mid + [(ROWS - 1, 1, NATW - W)]:
                 nc.vector.quantize_mx(
                     out=natq[b][:, pos : pos + nr * W].bitcast(FP8X4),
                     scales=nats[b][:, pos : pos + nr * W],
                     in_=gq[:, r0 * rw : (r0 + nr) * rw],
                 )
-            calls = [(0, 2, 0)]
-            calls.extend([(2 * u + 1, 2, TRI * u + 2 * W) for u in range(ROWS // 2 - 1)])
-            calls.append((ROWS - 2, 2, TRI * (ROWS // 2 - 1) + W))
-            for r0, nr, pos in calls:
+            for r0, nr, pos in [(0, 2, W)] + mid + [(ROWS - 2, 2, NATW - 2 * W)]:
                 nc.vector.quantize_mx(
-                    out=natk[b][:, pos : pos + nr * W].bitcast(FP8X4),
+                    out=natk[b][:, W + r0 * W : W + (r0 + nr) * W].bitcast(FP8X4),
                     scales=nats[b][4:P, pos : pos + nr * W],
                     in_=gk[:, r0 * rw : (r0 + nr) * rw],
                 )
 
-        def new_head(n):
-            d = {}
-            d["p"] = pp.tile([P, H // 2, P], F32, name="prob", tag="prob")
-            for nm in ("nmw", "sw", "nm", "sh"):
-                d[nm] = stat.tile([P, H // 2], F32, name=nm, tag=nm)
-            d["f"] = stat.tile([P, H // 2, 2], F32, name="fac", tag="fac")
-            head[n] = d
-
-        def row_energies(t):
-            n, c = divmod(t, NCHUNK)
-            if c == 0:
-                new_head(n)
-            d = head[n]
-            b = t % NB
-            banks = []
-            for u in range(ROWS // 2):
-                if u % 4 == 0:
-                    ew = psum.tile([P, 4, P], F32, name="ew", tag="bank")
-                    banks.append(ew)
-                a = TRI * u
-                nc.tensor.matmul_mx(
-                    out=ew[:, u % 4, :],
-                    lhsT=natq[b][:, a : a + P].bitcast(FP8X4),
-                    lhsT_scale=nats[b][:, a : a + P],
-                    rhs=natk[b][:, a : a + P].bitcast(FP8X4),
-                    rhs_scale=nats[b][4:P, a : a + P],
-                    start=True,
-                    stop=False,
-                )
-                nc.tensor.matmul_mx(
-                    out=ew[:, u % 4, :],
-                    lhsT=natq[b][:, a + W : a + W + P].bitcast(FP8X4),
-                    lhsT_scale=nats[b][:, a + W : a + W + P],
-                    rhs=natk[b][:, a + 2 * W : a + 2 * W + P].bitcast(FP8X4),
-                    rhs_scale=nats[b][4:P, a + 2 * W : a + 2 * W + P],
-                    start=False,
-                    stop=True,
-                )
-            d["ew%d" % c] = banks
-
         def moves(t):
-            n, c = divmod(t, NCHUNK)
-            b = t % NB
-            m = n % 2
+            c = t % NCHUNK
+            b = t % RING
             h0 = c * ROWS
             wstep = W // 4 if t == NSTEP - 1 else W
             for w0 in range(0, W, wstep):
-                for src, dst in ((natq[b], movq[m]), (natk[b], movk[m]), (nats[b], movs[m])):
-                    sv = src[:, 0 : NATW - W].rearrange("p (g u x w) -> p g u x w", g=4, u=2, x=3)[:, :, :, 0:3:2, w0 : w0 + wstep]
+                for src, dst in ((natq[b], movq), (natk[b], movk), (nats[b], movs)):
+                    if dst is movk:
+                        sv = src[:, W:NATKW].rearrange("p (g u v w) -> p g u v w", g=4, u=2, v=2)[:, :, :, :, w0 : w0 + wstep]
+                    else:
+                        sv = src[:, W:NATW].rearrange("p (g u x w) -> p g u x w", g=4, u=2, x=3)[:, :, :, 0:3:2, w0 : w0 + wstep]
                     dv = dst[:, 0 : H * W].rearrange("p (w h) -> p w h", h=H)[:, w0 : w0 + wstep, h0 : h0 + ROWS]
                     nc.vector.tensor_copy(
                         out=dv.rearrange("p w (g u v) -> p g w u v", g=4, u=2),
                         in_=sv.rearrange("p g u v w -> p g w u v"),
                     )
 
-        def row_softmax(t):
-            n, c = divmod(t, NCHUNK)
-            d = head[n]
-            banks = d["ew%d" % c]
-            s0 = c * (ROWS // 2)
-            mwt = stat.tile([P, ROWS // 2], F32, name="mwt", tag="mwt")
-            for i, ew in enumerate(banks):
-                nc.vector.tensor_reduce(out=mwt[:, 4 * i : 4 * i + 4], in_=ew[:, :, 0:W], axis=AX.X, op=ALU.max)
-            nc.vector.tensor_scalar(out=d["nmw"][:, s0 : s0 + ROWS // 2], in0=mwt[:], scalar1=-1.0, scalar2=None, op0=ALU.mult)
-            for u in range(ROWS // 2):
-                s = s0 + u
-                nc.scalar.activation(
-                    out=d["p"][:, s, W:P],
-                    in_=banks[u // 4][:, u % 4, 0:W],
-                    func=ACT.Exp,
-                    bias=d["nmw"][:, s : s + 1],
-                    scale=1.0,
-                    accum_out=d["sw"][:, s : s + 1],
-                )
-
         def col_energies(n):
-            m = n % 2
             for wq in range(W // 4):
                 eh = psum.tile([P, 4, P], F32, name="eh", tag="bank")
                 for i in range(4):
                     a = (4 * wq + i) * H
                     nc.tensor.matmul_mx(
                         out=eh[:, i, :],
-                        lhsT=movk[m][:, a : a + P].bitcast(FP8X4),
-                        lhsT_scale=movs[m][4:P, a : a + P],
-                        rhs=movq[m][:, a : a + P].bitcast(FP8X4),
-                        rhs_scale=movs[m][:, a : a + P],
+                        lhsT=movk[:, a : a + P].bitcast(FP8X4),
+                        lhsT_scale=movs[4:P, a : a + P],
+                        rhs=movq[:, a : a + P].bitcast(FP8X4),
+                        rhs_scale=movs[:, a : a + P],
                         start=True,
                         stop=True,
                     )
-                if n == NH - 1 and wq % 2 == 1:
-                    nc.vector.tensor_copy(out=s2v[:, :, 4 * wq : 4 * wq + 4], in_=eh[:, :, 0:H].rearrange("p w h -> p h w"))
+                if n == NH - 1:
+                    nc.vector.tensor_tensor(
+                        out=s2v[:, :, 4 * wq : 4 * wq + 4],
+                        in0=eh[:, :, 0:H].rearrange("p w h -> p h w"),
+                        in1=maskj[:].unsqueeze(2).to_broadcast([P, H, 4]),
+                        op=ALU.add,
+                    )
                 else:
                     nc.scalar.copy(out=s2v[:, :, 4 * wq : 4 * wq + 4], in_=eh[:, :, 0:H].rearrange("p w h -> p h w"))
 
-        def col_softmax(n, banks):
-            d = head[n]
-            for sq in banks:
-                et = psum.tile([P, 4, P], F32, name="et", tag="bank")
-                for i in range(4):
-                    s = 4 * sq + i
-                    nc.tensor.matmul(out=et[:, i, :], lhsT=s2[:, P * s : P * (s + 1)], rhs=w2[:, 0:P], is_transpose=True, start=True, stop=False)
-                    nc.tensor.matmul(out=et[:, i, :], lhsT=cmask[:], rhs=w2[:, P - 2 * s : 2 * P - 2 * s], is_transpose=True, start=False, stop=True)
-                mht = stat.tile([P, 4], F32, name="mht", tag="mht")
-                nc.vector.tensor_reduce(out=mht[:], in_=et[:, :, 0:H], axis=AX.X, op=ALU.max)
-                nc.vector.scalar_tensor_tensor(
-                    out=d["nm"][:, 4 * sq : 4 * sq + 4], in0=mht[:], scalar=-1.0, in1=d["nmw"][:, 4 * sq : 4 * sq + 4], op0=ALU.mult, op1=ALU.min
+        def bank_rows(n, bk):
+            s0 = 3 * bk
+            ns = min(3, H // 2 - s0)
+            ps = psum.tile([P, 4 * P], F32, name="ps", tag="bank")
+            banks[(n, bk)] = ps
+            for i in reversed(range(ns)):
+                s = s0 + i
+                b = (n * NCHUNK + s // (ROWS // 2)) % RING
+                a = W + TRI * (s % (ROWS // 2))
+                ka = 2 * W * (s % (ROWS // 2))
+                o = 3 * W + W * i
+                nc.tensor.matmul_mx(
+                    out=ps[:, o : o + P],
+                    lhsT=natq[b][:, a : a + P].bitcast(FP8X4),
+                    lhsT_scale=nats[b][:, a : a + P],
+                    rhs=natk[b][:, ka : ka + P].bitcast(FP8X4),
+                    rhs_scale=nats[b][4:P, a - W : a - W + P],
+                    start=True,
+                    stop=False,
                 )
-                for i in range(4):
-                    s = 4 * sq + i
-                    nc.scalar.activation(
-                        out=d["p"][:, s, 0:H],
-                        in_=et[:, i, 0:H],
-                        func=ACT.Exp,
-                        bias=d["nm"][:, s : s + 1],
-                        scale=1.0,
-                        accum_out=d["sh"][:, s : s + 1],
-                    )
+                nc.tensor.matmul_mx(
+                    out=ps[:, o : o + P],
+                    lhsT=natq[b][:, a + W : a + W + P].bitcast(FP8X4),
+                    lhsT_scale=nats[b][:, a + W : a + W + P],
+                    rhs=natk[b][:, ka + W : ka + W + P].bitcast(FP8X4),
+                    rhs_scale=nats[b][4:P, a + W : a + W + P],
+                    start=False,
+                    stop=True,
+                )
 
-        def factors(n, s0, ns):
-            d = head[n]
-            sl = slice(s0, s0 + ns)
-            dw = stat.tile([P, 16], F32, name="dw", tag="dw")
-            ef = stat.tile([P, 16], F32, name="ef", tag="ef")
-            tot = stat.tile([P, 16], F32, name="tot", tag="tot")
-            nc.vector.tensor_tensor(out=dw[:, 0:ns], in0=d["nm"][:, sl], in1=d["nmw"][:, sl], op=ALU.subtract)
-            nc.scalar.activation(out=ef[:, 0:ns], in_=dw[:, 0:ns], func=ACT.Exp)
-            nc.vector.tensor_tensor(out=tot[:, 0:ns], in0=d["sw"][:, sl], in1=ef[:, 0:ns], op=ALU.mult)
-            nc.vector.tensor_tensor(out=tot[:, 0:ns], in0=tot[:, 0:ns], in1=d["sh"][:, sl], op=ALU.add)
-            nc.vector.reciprocal(out=d["f"][:, sl, 0], in_=tot[:, 0:ns])
-            nc.vector.tensor_tensor(out=d["f"][:, sl, 1], in0=ef[:, 0:ns], in1=d["f"][:, sl, 0], op=ALU.mult)
+        def bank_rest(n, bk):
+            s0 = 3 * bk
+            ns = min(3, H // 2 - s0)
+            ps = banks[(n, bk)]
+            for i in range(ns):
+                s = s0 + i
+                if n == NH - 1:
+                    nc.tensor.transpose(ps[:, W * i : W * i + P], s2[:, P * s : P * (s + 1)], w2[:, 0:P])
+                else:
+                    nc.tensor.matmul(out=ps[:, W * i : W * i + P], lhsT=s2[:, P * s : P * (s + 1)], rhs=w2[:, 0:P], is_transpose=True, start=True, stop=False)
+                    nc.tensor.matmul(out=ps[:, W * i : W * i + P], lhsT=cmask[:], rhs=w2[:, P - 2 * s : 2 * P - 2 * s], is_transpose=True, start=False, stop=True)
+            pv = ps[:].rearrange("p (c x j) -> p c x j", c=2, x=4)
+            if bk % 2 == 0:
+                prob[(n, bk // 2)] = pp.tile([P, 6, P], F32, name="prob", tag="prob")
+            if bk == 0:
+                sums[n] = stat.tile([P, H // 2], F32, name="sums", tag="sums", bufs=2)
+            pt = prob[(n, bk // 2)]
+            o = 3 * (bk % 2)
+            mx = stat.tile([P, 4], F32, name="mx", tag="mx")
+            nm = stat.tile([P, 4], F32, name="nm", tag="nm")
+            nc.vector.tensor_reduce(out=mx[:, 0:ns], in_=pv[:, :, 0:ns, :].rearrange("p c x j -> p x c j"), axis=AX.XY, op=ALU.max)
+            nc.vector.tensor_scalar(out=nm[:, 0:ns], in0=mx[:, 0:ns], scalar1=-1.0, scalar2=None, op0=ALU.mult)
+            for i in range(ns):
+                nc.scalar.activation(
+                    out=pt[:, o + i, :].rearrange("p (c j) -> p c j", c=2),
+                    in_=pv[:, :, i, :],
+                    func=ACT.Exp,
+                    bias=nm[:, i : i + 1],
+                    scale=1.0,
+                    accum_out=sums[n][:, s0 + i : s0 + i + 1],
+                )
 
-        def finish(n, s0, ns, on_vector):
-            d = head[n]
-            pr = d["p"]
-            sl = slice(s0, s0 + ns)
-            if on_vector:
-                pv = pr[:, sl, :].rearrange("p s (f j) -> p (s f) j", f=2)
-                fv = d["f"][:, sl, :].rearrange("p s f -> p (s f)").unsqueeze(2).to_broadcast([P, 2 * ns, W])
-                nc.vector.tensor_tensor(out=pv, in0=pv, in1=fv, op=ALU.mult)
+        def pair_recip(n, pr):
+            first = 6 * pr
+            cnt = min(6, H // 2 - first)
+            if pr == 0:
+                recs[n] = stat.tile([P, H // 2], F32, name="recs", tag="recs", bufs=2)
+            nc.vector.reciprocal(out=recs[n][:, first : first + cnt], in_=sums[n][:, first : first + cnt])
+
+        def pair_out(n, pr):
+            first = 6 * pr
+            cnt = min(6, H // 2 - first)
+            pt = prob[(n, pr)]
+            for i in range(cnt):
+                nc.scalar.activation(out=pt[:, i, :], in_=pt[:, i, :], func=ACT.Copy, scale=recs[n][:, first + i : first + i + 1])
+            nc.sync.dma_start(out=o0v[n, :, first : first + cnt, :], in_=pt[:, 0:cnt, :])
+            f8 = f8p.tile([P, 6, P], FP8, name="f8", tag="f8")
+            if n == 1:
+                nc.scalar.activation(out=f8[:, 0:cnt, :], in_=pt[:, 0:cnt, :], func=ACT.Copy, scale=Y_SCALE, saturate=False)
             else:
-                for s in range(s0, s0 + ns):
-                    for hf in range(2):
-                        nc.scalar.activation(
-                            out=pr[:, s, hf * W : (hf + 1) * W],
-                            in_=pr[:, s, hf * W : (hf + 1) * W],
-                            func=ACT.Copy,
-                            scale=d["f"][:, s, hf : hf + 1],
-                        )
-            nc.sync.dma_start(out=o0v[n, :, sl, :], in_=pr[:, sl, :])
-            f8 = f8p.tile([P, 16, P], FP8, name="f8", tag="f8")
-            nc.vector.tensor_scalar(out=f8[:, 0:ns, :], in0=pr[:, sl, :], scalar1=Y_SCALE, scalar2=None, op0=ALU.mult, saturate=False)
-            for i in range(ns // 4):
-                s = s0 + 4 * i
-                nc.sync.dma_start(out=o1v[n, :, s : s + 4, :], in_=f8[:, 4 * i : 4 * i + 4, :].bitcast(U8))
+                nc.vector.tensor_scalar(out=f8[:, 0:cnt, :], in0=pt[:, 0:cnt, :], scalar1=Y_SCALE, scalar2=None, op0=ALU.mult, saturate=False)
+            for a in range(0, cnt, 3):
+                e = min(a + 3, cnt)
+                nc.sync.dma_start(out=o1v[n, :, first + a : first + e, :], in_=f8[:, a:e, :].bitcast(U8))
 
         load(0)
         load(1)
         interleave(0)
+        plan = {0: (0, 1, 2, 3), 1: (4, 5, 6, 7), 2: (8, 9, 10)}
         for t in range(NSTEP):
             if t + 2 < NSTEP:
                 load(t + 2)
             if t + 1 < NSTEP:
                 interleave(t + 1)
             quantise(t)
-            row_energies(t)
+            if t + 2 < RING:
+                init_ring(t + 2)
             moves(t)
-            row_softmax(t)
-            n, e = divmod(t - NCHUNK, NCHUNK)
-            if n >= 0:
-                if e == 0:
-                    col_energies(n)
-                elif e == 1:
-                    col_softmax(n, range(0, 4))
-                    factors(n, 0, 16)
-                elif e == 2:
-                    finish(n, 0, 16, False)
-                    col_softmax(n, range(4, 8))
-                    factors(n, 16, 16)
-                elif n == 0:
-                    finish(n, 16, 16, False)
-        n = NH - 1
-        col_energies(n)
-        finish(n - 1, 16, 16, False)
-        for g in range(4):
-            col_softmax(n, range(2 * g, 2 * g + 2))
-            factors(n, 8 * g, 8)
-            finish(n, 8 * g, 8, False)
+            n, e = divmod(t, NCHUNK)
+            if t == NSTEP - 1:
+                for bk in range(AHEAD):
+                    bank_rows(n, bk)
+            if e == NCHUNK - 1:
+                col_energies(n)
+            if t == NSTEP - 1:
+                for pr in range(6):
+                    pair_out(1, pr)
+            if n >= 1:
+                for bk in plan.get(e, ()):
+                    bank_rows(n - 1, bk)
+                    bank_rest(n - 1, bk)
+                    if bk % 2 == 1 or bk == 10:
+                        pair_recip(n - 1, bk // 2)
+                        if n == 1:
+                            pair_out(0, bk // 2)
+        for bk in range(11):
+            if bk + AHEAD < 11:
+                bank_rows(NH - 1, bk + AHEAD)
+            bank_rest(NH - 1, bk)
+            if bk % 2 == 1 or bk == 10:
+                pair_recip(NH - 1, bk // 2)
+                pair_out(NH - 1, bk // 2)

@@ -25,9 +25,9 @@ TRI = 3 * W
 NATW = W + (ROWS // 2) * TRI
 NATKW = W + CH
 MOVW = H * W + W
-XV = 432
+XV = 456
 XV0 = 768
-XV1 = 304
+XV1 = 328
 RING = 6
 AHEAD = 4
 NEG = -1.0e9
@@ -231,10 +231,8 @@ def tile_multiheadcrisscrossattention_pa_kernel(tc, q, k, out_0, out_1):
                 sums[n] = stat.tile([P, H // 2], F32, name="sums", tag="sums", bufs=2)
             pt = prob[(n, bk // 2)]
             o = 3 * (bk % 2)
-            mx = stat.tile([P, 4], F32, name="mx", tag="mx")
             nm = stat.tile([P, 4], F32, name="nm", tag="nm")
-            nc.vector.tensor_reduce(out=mx[:, 0:ns], in_=pv[:, :, 0:ns, :].rearrange("p c x j -> p x c j"), axis=AX.XY, op=ALU.max)
-            nc.vector.tensor_scalar(out=nm[:, 0:ns], in0=mx[:, 0:ns], scalar1=-1.0, scalar2=None, op0=ALU.mult)
+            nc.vector.tensor_reduce(out=nm[:, 0:ns], in_=pv[:, :, 0:ns, :].rearrange("p c x j -> p x c j"), axis=AX.XY, op=ALU.max, negate=True)
             for i in range(ns):
                 nc.scalar.activation(
                     out=pt[:, o + i, :].rearrange("p (c j) -> p c j", c=2),
@@ -271,6 +269,8 @@ def tile_multiheadcrisscrossattention_pa_kernel(tc, q, k, out_0, out_1):
         load(0)
         load(1)
         interleave(0)
+        for b in range(2, RING):
+            init_ring(b)
         plan = {0: (0, 1, 2, 3), 1: (4, 5, 6, 7), 2: (8, 9, 10)}
         for t in range(NSTEP):
             if t + 2 < NSTEP:
@@ -278,8 +278,6 @@ def tile_multiheadcrisscrossattention_pa_kernel(tc, q, k, out_0, out_1):
             if t + 1 < NSTEP:
                 interleave(t + 1)
             quantise(t)
-            if t + 2 < RING:
-                init_ring(t + 2)
             moves(t)
             n, e = divmod(t, NCHUNK)
             if t == NSTEP - 1:

@@ -68,7 +68,7 @@ def tile_multiheadcrisscrossattention_pa_kernel(tc, q, k, out_0, out_1):
         for b in range(RING):
             tq = keep.tile([P, NATW], I32, name="natq%d" % b, align_bytes=64)
             tk = keep.tile([P, NATKW], I32, name="natk%d" % b, align_bytes=64)
-            ts = keep.tile([P, NATW], U8, name="nats%d" % b, align_bytes=64)
+            ts = keep.tile([P, NATKW], U8, name="nats%d" % b, align_bytes=64)
             natq.append(tq)
             natk.append(tk)
             nats.append(ts)
@@ -76,7 +76,6 @@ def tile_multiheadcrisscrossattention_pa_kernel(tc, q, k, out_0, out_1):
         def init_ring(b):
             sv = nats[b][:].bitcast(I32)
             nc.vector.memset(natq[b][:, W:NATW].rearrange("p (u x w) -> p u x w", x=3, w=W)[:, :, 1, :], 0)
-            nc.vector.memset(sv[:, W // 4 : NATW // 4].rearrange("p (u x w) -> p u x w", x=3, w=W // 4)[:, :, 1, :], 0)
             nc.vector.memset(sv[:, 0 : W // 4], 0)
             nc.vector.memset(natk[b][:, 0:W], 0)
 
@@ -132,13 +131,14 @@ def tile_multiheadcrisscrossattention_pa_kernel(tc, q, k, out_0, out_1):
             for r0, nr, pos in [(0, 1, W)] + mid + [(ROWS - 1, 1, NATW - W)]:
                 nc.vector.quantize_mx(
                     out=natq[b][:, pos : pos + nr * W].bitcast(FP8X4),
-                    scales=nats[b][:, pos : pos + nr * W],
+                    scales=nats[b][:, W + r0 * W : W + (r0 + nr) * W],
                     in_=gq[:, r0 * rw : (r0 + nr) * rw],
                 )
-            for r0, nr, pos in [(0, 2, W)] + mid + [(ROWS - 2, 2, NATW - 2 * W)]:
+            nr = ROWS // 2
+            for r0 in (0, nr):
                 nc.vector.quantize_mx(
                     out=natk[b][:, W + r0 * W : W + (r0 + nr) * W].bitcast(FP8X4),
-                    scales=nats[b][4:P, pos : pos + nr * W],
+                    scales=nats[b][4:P, W + r0 * W : W + (r0 + nr) * W],
                     in_=gk[:, r0 * rw : (r0 + nr) * rw],
                 )
 
@@ -149,7 +149,7 @@ def tile_multiheadcrisscrossattention_pa_kernel(tc, q, k, out_0, out_1):
             wstep = W // 4 if t == NSTEP - 1 else W
             for w0 in range(0, W, wstep):
                 for src, dst in ((natq[b], movq), (natk[b], movk), (nats[b], movs)):
-                    if dst is movk:
+                    if dst is not movq:
                         sv = src[:, W:NATKW].rearrange("p (g u v w) -> p g u v w", g=4, u=2, v=2)[:, :, :, :, w0 : w0 + wstep]
                     else:
                         sv = src[:, W:NATW].rearrange("p (g u x w) -> p g u x w", g=4, u=2, x=3)[:, :, :, 0:3:2, w0 : w0 + wstep]
@@ -197,18 +197,18 @@ def tile_multiheadcrisscrossattention_pa_kernel(tc, q, k, out_0, out_1):
                 nc.tensor.matmul_mx(
                     out=ps[:, o : o + P],
                     lhsT=natq[b][:, a : a + P].bitcast(FP8X4),
-                    lhsT_scale=nats[b][:, a : a + P],
+                    lhsT_scale=nats[b][:, ka + W : ka + W + P],
                     rhs=natk[b][:, ka : ka + P].bitcast(FP8X4),
-                    rhs_scale=nats[b][4:P, a - W : a - W + P],
+                    rhs_scale=nats[b][4:P, ka : ka + P],
                     start=True,
                     stop=False,
                 )
                 nc.tensor.matmul_mx(
                     out=ps[:, o : o + P],
                     lhsT=natq[b][:, a + W : a + W + P].bitcast(FP8X4),
-                    lhsT_scale=nats[b][:, a + W : a + W + P],
+                    lhsT_scale=nats[b][:, ka + W : ka + W + P],
                     rhs=natk[b][:, ka + W : ka + W + P].bitcast(FP8X4),
-                    rhs_scale=nats[b][4:P, a + W : a + W + P],
+                    rhs_scale=nats[b][4:P, ka + W : ka + W + P],
                     start=False,
                     stop=True,
                 )
@@ -255,7 +255,10 @@ def tile_multiheadcrisscrossattention_pa_kernel(tc, q, k, out_0, out_1):
             cnt = min(6, H // 2 - first)
             pt = prob[(n, pr)]
             for i in range(cnt):
-                nc.scalar.activation(out=pt[:, i, :], in_=pt[:, i, :], func=ACT.Copy, scale=recs[n][:, first + i : first + i + 1])
+                if n == NH - 1:
+                    nc.vector.tensor_scalar(out=pt[:, i, :], in0=pt[:, i, :], scalar1=recs[n][:, first + i : first + i + 1], scalar2=None, op0=ALU.mult)
+                else:
+                    nc.scalar.activation(out=pt[:, i, :], in_=pt[:, i, :], func=ACT.Copy, scale=recs[n][:, first + i : first + i + 1])
             nc.sync.dma_start(out=o0v[n, :, first : first + cnt, :], in_=pt[:, 0:cnt, :])
             f8 = f8p.tile([P, 6, P], FP8, name="f8", tag="f8")
             if n == 1:

@@ -25,9 +25,9 @@ TRI = 3 * W
 NATW = W + (ROWS // 2) * TRI
 NATKW = W + CH
 MOVW = H * W + W
-XV = 456
+XV = 496
 XV0 = 768
-XV1 = 328
+XV1 = 368
 RING = 6
 AHEAD = 4
 NEG = -1.0e9

@@ -154,10 +154,16 @@ def tile_multiheadcrisscrossattention_pa_kernel(tc, q, k, out_0, out_1):
                     else:
                         sv = src[:, W:NATW].rearrange("p (g u x w) -> p g u x w", g=4, u=2, x=3)[:, :, :, 0:3:2, w0 : w0 + wstep]
                     dv = dst[:, 0 : H * W].rearrange("p (w h) -> p w h", h=H)[:, w0 : w0 + wstep, h0 : h0 + ROWS]
-                    nc.vector.tensor_copy(
-                        out=dv.rearrange("p w (g u v) -> p g w u v", g=4, u=2),
-                        in_=sv.rearrange("p g u v w -> p g w u v"),
-                    )
+                    if dst is movs:
+                        nc.vector.tensor_copy(
+                            out=dv.rearrange("p (a i) (g r) -> p a g i r", i=4, g=4),
+                            in_=src[:, W:NATKW].rearrange("p (g r w) -> p g r w", g=4, r=4)[:, :, :, w0 : w0 + wstep].rearrange("p g r (a i) -> p a g i r", i=4),
+                        )
+                    else:
+                        nc.vector.tensor_copy(
+                            out=dv.rearrange("p w (g u v) -> p g w u v", g=4, u=2),
+                            in_=sv.rearrange("p g u v w -> p g w u v"),
+                        )
 
         def col_energies(n):
             for wq in range(W // 4):

@@ -45,7 +45,7 @@ def tile_multiheadcrisscrossattention_pa_kernel(tc, q, k, out_0, out_1):
         const = ctx.enter_context(tc.tile_pool(name="const", bufs=1))
         keep = ctx.enter_context(tc.tile_pool(name="keep", bufs=1))
         rawp = ctx.enter_context(tc.tile_pool(name="rawp", bufs=4))
-        gp = ctx.enter_context(tc.tile_pool(name="gp", bufs=4))
+        gp = ctx.enter_context(tc.tile_pool(name="gp", bufs=6))
         pp = ctx.enter_context(tc.tile_pool(name="pp", bufs=9))
         f8p = ctx.enter_context(tc.tile_pool(name="f8p", bufs=3))
         stat = ctx.enter_context(tc.tile_pool(name="stat", bufs=4))
@@ -108,7 +108,7 @@ def tile_multiheadcrisscrossattention_pa_kernel(tc, q, k, out_0, out_1):
                     nc.sync.dma_start(out=raws[(t, nm)][:, :, i * pw : (i + 1) * pw], in_=src[n, :, :, c * CH + i * pw : c * CH + (i + 1) * pw])
 
         def interleave(t):
-            xv = XV0 if t == 0 else (XV1 if t <= NCHUNK else XV)
+            xv = XV0 if t == 0 else (XV1 if t <= NCHUNK + 1 else XV)
             step = 256 if t == 0 else CH
             for nm in ("q", "k"):
                 gs[(t, nm)] = gp.tile([P, 4 * CH], BF16, name="g", tag="g", align_bytes=64)
@@ -150,9 +150,9 @@ def tile_multiheadcrisscrossattention_pa_kernel(tc, q, k, out_0, out_1):
             for w0 in range(0, W, wstep):
                 for src, dst in ((natq[b], movq), (natk[b], movk), (nats[b], movs)):
                     if dst is not movq:
-                        sv = src[:, W:NATKW].rearrange("p (g u v w) -> p g u v w", g=4, u=2, v=2)[:, :, :, :, w0 : w0 + wstep]
+                        sv = src[:, W:NATKW].rearrange("p (u v w) -> p u v w", u=ROWS // 2, v=2)[:, :, :, w0 : w0 + wstep]
                     else:
-                        sv = src[:, W:NATW].rearrange("p (g u x w) -> p g u x w", g=4, u=2, x=3)[:, :, :, 0:3:2, w0 : w0 + wstep]
+                        sv = src[:, W:NATW].rearrange("p (u x w) -> p u x w", u=ROWS // 2, x=3)[:, :, 0:3:2, w0 : w0 + wstep]
                     dv = dst[:, 0 : H * W].rearrange("p (w h) -> p w h", h=H)[:, w0 : w0 + wstep, h0 : h0 + ROWS]
                     if dst is movs:
                         nc.vector.tensor_copy(
@@ -161,8 +161,8 @@ def tile_multiheadcrisscrossattention_pa_kernel(tc, q, k, out_0, out_1):
                         )
                     else:
                         nc.vector.tensor_copy(
-                            out=dv.rearrange("p w (g u v) -> p g w u v", g=4, u=2),
-                            in_=sv.rearrange("p g u v w -> p g w u v"),
+                            out=dv.rearrange("p (a i) (u v) -> p a u i v", i=4, v=2),
+                            in_=sv.rearrange("p u v (a i) -> p a u i v", i=4),
                         )
 
         def col_energies(n):
@@ -280,12 +280,14 @@ def tile_multiheadcrisscrossattention_pa_kernel(tc, q, k, out_0, out_1):
         interleave(0)
         for b in range(2, RING):
             init_ring(b)
+        load(2)
+        interleave(1)
         plan = {0: (0, 1, 2, 3), 1: (4, 5, 6, 7), 2: (8, 9, 10)}
         for t in range(NSTEP):
+            if t + 3 < NSTEP:
+                load(t + 3)
             if t + 2 < NSTEP:
-                load(t + 2)
-            if t + 1 < NSTEP:
-                interleave(t + 1)
+                interleave(t + 2)
             quantise(t)
             moves(t)
             n, e = divmod(t, NCHUNK)

@@ -120,7 +120,9 @@ def tile_multiheadcrisscrossattention_pa_kernel(tc, q, k, out_0, out_1):
                     if a < xv:
                         nc.vector.tensor_copy(out=gv[:, a // 4 : min(b, xv) // 4, :, :], in_=rv[:, a // 4 : min(b, xv) // 4, :, :])
                     if b > xv:
-                        nc.scalar.copy(out=gv[:, max(a, xv) // 4 : b // 4, :, :], in_=rv[:, max(a, xv) // 4 : b // 4, :, :])
+                        gw = gs[(t, nm)][:].rearrange("p (c i t) -> p c t i", i=8, t=4)
+                        rw = raws[(t, nm)][:].rearrange("p t (c i) -> p c t i", i=8)
+                        nc.scalar.copy(out=gw[:, max(a, xv) // 8 : b // 8, :, :], in_=rw[:, max(a, xv) // 8 : b // 8, :, :])
 
         def quantise(t):
             b = t % RING

@@ -114,15 +114,13 @@ def tile_multiheadcrisscrossattention_pa_kernel(tc, q, k, out_0, out_1):
                 gs[(t, nm)] = gp.tile([P, 4 * CH], BF16, name="g", tag="g", align_bytes=64)
             for a in range(0, CH, step):
                 for nm in ("q", "k"):
-                    gv = gs[(t, nm)][:].rearrange("p (c i t) -> p c t i", i=4, t=4)
-                    rv = raws[(t, nm)][:].rearrange("p t (c i) -> p c t i", i=4)
+                    gv = gs[(t, nm)][:].rearrange("p (c i t) -> p c t i", i=8, t=4)
+                    rv = raws[(t, nm)][:].rearrange("p t (c i) -> p c t i", i=8)
                     b = min(a + step, CH)
                     if a < xv:
-                        nc.vector.tensor_copy(out=gv[:, a // 4 : min(b, xv) // 4, :, :], in_=rv[:, a // 4 : min(b, xv) // 4, :, :])
+                        nc.vector.tensor_copy(out=gv[:, a // 8 : min(b, xv) // 8, :, :], in_=rv[:, a // 8 : min(b, xv) // 8, :, :])
                     if b > xv:
-                        gw = gs[(t, nm)][:].rearrange("p (c i t) -> p c t i", i=8, t=4)
-                        rw = raws[(t, nm)][:].rearrange("p t (c i) -> p c t i", i=8)
-                        nc.scalar.copy(out=gw[:, max(a, xv) // 8 : b // 8, :, :], in_=rw[:, max(a, xv) // 8 : b // 8, :, :])
+                        nc.scalar.copy(out=gv[:, max(a, xv) // 8 : b // 8, :, :], in_=rv[:, max(a, xv) // 8 : b // 8, :, :])
 
         def quantise(t):
             b = t % RING

@@ -120,7 +120,9 @@ def tile_multiheadcrisscrossattention_pa_kernel(tc, q, k, out_0, out_1):
                     if a < xv:
                         nc.vector.tensor_copy(out=gv[:, a // 8 : min(b, xv) // 8, :, :], in_=rv[:, a // 8 : min(b, xv) // 8, :, :])
                     if b > xv:
-                        nc.scalar.copy(out=gv[:, max(a, xv) // 8 : b // 8, :, :], in_=rv[:, max(a, xv) // 8 : b // 8, :, :])
+                        gw = gs[(t, nm)][:].rearrange("p (c i y z) -> p c y i z", i=8, y=2, z=2)
+                        rw = raws[(t, nm)][:].rearrange("p (y z) (c i) -> p c y i z", i=8, z=2)
+                        nc.scalar.copy(out=gw[:, max(a, xv) // 8 : b // 8, :, :, :], in_=rw[:, max(a, xv) // 8 : b // 8, :, :, :])
 
         def quantise(t):
             b = t % RING

@@ -114,15 +114,13 @@ def tile_multiheadcrisscrossattention_pa_kernel(tc, q, k, out_0, out_1):
                 gs[(t, nm)] = gp.tile([P, 4 * CH], BF16, name="g", tag="g", align_bytes=64)
             for a in range(0, CH, step):
                 for nm in ("q", "k"):
-                    gv = gs[(t, nm)][:].rearrange("p (c i t) -> p c t i", i=8, t=4)
-                    rv = raws[(t, nm)][:].rearrange("p t (c i) -> p c t i", i=8)
+                    gv = gs[(t, nm)][:].rearrange("p (c i y z) -> p c y i z", i=8, y=2, z=2)
+                    rv = raws[(t, nm)][:].rearrange("p (y z) (c i) -> p c y i z", i=8, z=2)
                     b = min(a + step, CH)
                     if a < xv:
-                        nc.vector.tensor_copy(out=gv[:, a // 8 : min(b, xv) // 8, :, :], in_=rv[:, a // 8 : min(b, xv) // 8, :, :])
+                        nc.vector.tensor_copy(out=gv[:, a // 8 : min(b, xv) // 8, :, :, :], in_=rv[:, a // 8 : min(b, xv) // 8, :, :, :])
                     if b > xv:
-                        gw = gs[(t, nm)][:].rearrange("p (c i y z) -> p c y i z", i=8, y=2, z=2)
-                        rw = raws[(t, nm)][:].rearrange("p (y z) (c i) -> p c y i z", i=8, z=2)
-                        nc.scalar.copy(out=gw[:, max(a, xv) // 8 : b // 8, :, :, :], in_=rw[:, max(a, xv) // 8 : b // 8, :, :, :])
+                        nc.scalar.copy(out=gv[:, max(a, xv) // 8 : b // 8, :, :, :], in_=rv[:, max(a, xv) // 8 : b // 8, :, :, :])
 
         def quantise(t):
             b = t % RING

@@ -156,8 +156,8 @@ def tile_multiheadcrisscrossattention_pa_kernel(tc, q, k, out_0, out_1):
                     dv = dst[:, 0 : H * W].rearrange("p (w h) -> p w h", h=H)[:, w0 : w0 + wstep, h0 : h0 + ROWS]
                     if dst is movs:
                         nc.vector.tensor_copy(
-                            out=dv.rearrange("p (a i) (g r) -> p a g i r", i=4, g=4),
-                            in_=src[:, W:NATKW].rearrange("p (g r w) -> p g r w", g=4, r=4)[:, :, :, w0 : w0 + wstep].rearrange("p g r (a i) -> p a g i r", i=4),
+                            out=dv.rearrange("p (a i) (g r) -> p a g i r", i=4, g=8),
+                            in_=src[:, W:NATKW].rearrange("p (g r w) -> p g r w", g=8, r=2)[:, :, :, w0 : w0 + wstep].rearrange("p g r (a i) -> p a g i r", i=4),
                         )
                     else:
                         nc.vector.tensor_copy(

@@ -30,6 +30,7 @@ XV0 = 768
 XV1 = 368
 RING = 6
 AHEAD = 4
+WARM = 14
 NEG = -1.0e9
 Y_SCALE = 12000.0
 
@@ -168,6 +169,19 @@ def tile_multiheadcrisscrossattention_pa_kernel(tc, q, k, out_0, out_1):
         def col_energies(n):
             for wq in range(W // 4):
                 eh = psum.tile([P, 4, P], F32, name="eh", tag="bank")
+                if wq == 0:
+                    b = (n * NCHUNK + NCHUNK - 1) % RING
+                    bo = (b - 1) % RING
+                    for d in range(WARM):
+                        nc.tensor.matmul_mx(
+                            out=eh[:, d % 4, :],
+                            lhsT=natq[b][:, W : W + P].bitcast(FP8X4),
+                            lhsT_scale=nats[bo][:, W : W + P],
+                            rhs=natk[bo][:, W : W + P].bitcast(FP8X4),
+                            rhs_scale=nats[bo][4:P, W : W + P],
+                            start=True,
+                            stop=True,
+                        )
                 for i in range(4):
                     a = (4 * wq + i) * H
                     nc.tensor.matmul_mx(

@@ -25,9 +25,9 @@ TRI = 3 * W
 NATW = W + (ROWS // 2) * TRI
 NATKW = W + CH
 MOVW = H * W + W
-XV = 496
+XV = 512
 XV0 = 768
-XV1 = 368
+XV1 = 384
 RING = 6
 AHEAD = 4
 WARM = 14

@@ -25,9 +25,9 @@ TRI = 3 * W
 NATW = W + (ROWS // 2) * TRI
 NATKW = W + CH
 MOVW = H * W + W
-XV = 512
+XV = 528
 XV0 = 768
-XV1 = 384
+XV1 = 400
 RING = 6
 AHEAD = 4
 WARM = 14

from contextlib import ExitStack

import concourse.mybir as mybir
from concourse.masks import make_identity

NH, HD, H, W = 3, 512, 64, 64
FLOPS = 2 * NH * H * W * (H + W) * HD

F32 = mybir.dt.float32
BF16 = mybir.dt.bfloat16
I32 = mybir.dt.int32
U8 = mybir.dt.uint8
FP8X4 = mybir.dt.float8_e4m3fn_x4
FP8 = mybir.dt.float8_e4m3fn
ALU = mybir.AluOpType
ACT = mybir.ActivationFunctionType
AX = mybir.AxisListType

P = 128
ROWS = 16
CH = ROWS * W
NCHUNK = H // ROWS
NSTEP = NH * NCHUNK
TRI = 3 * W
NATW = W + (ROWS // 2) * TRI
NATKW = W + CH
MOVW = H * W + W
XV = 528
XV0 = 768
XV1 = 400
RING = 6
AHEAD = 4
WARM = 14
NEG = -1.0e9
Y_SCALE = 12000.0


def tile_multiheadcrisscrossattention_pa_kernel(tc, q, k, out_0, out_1):
    nc = tc.nc
    qv = q.rearrange("b n (p t) h w -> (b n) p t (h w)", t=4)
    kv = k.rearrange("b n (p t) h w -> (b n) p t (h w)", t=4)
    o0v = out_0.rearrange("b n h w j -> (b n) (h w) j").rearrange("n (s p) j -> n p s j", p=P)
    o1v = out_1.rearrange("b n h w j -> (b n) (h w) j").rearrange("n (s p) j -> n p s j", p=P)

    with ExitStack() as ctx:
        const = ctx.enter_context(tc.tile_pool(name="const", bufs=1))
        keep = ctx.enter_context(tc.tile_pool(name="keep", bufs=1))
        rawp = ctx.enter_context(tc.tile_pool(name="rawp", bufs=4))
        gp = ctx.enter_context(tc.tile_pool(name="gp", bufs=6))
        pp = ctx.enter_context(tc.tile_pool(name="pp", bufs=9))
        f8p = ctx.enter_context(tc.tile_pool(name="f8p", bufs=3))
        stat = ctx.enter_context(tc.tile_pool(name="stat", bufs=4))
        psum = ctx.enter_context(tc.psum_pool(name="psum", bufs=8))

        w2 = const.tile([P, 2 * P], F32, name="w2")
        make_identity(nc, w2[:, 0:P])
        make_identity(nc, w2[:, P : 2 * P])
        cmask = const.tile([P, P], F32, name="cmask")
        nc.vector.tensor_scalar(out=cmask[:, 0:W], in0=w2[:, 0:1].to_broadcast([P, W]), scalar1=NEG, scalar2=None, op0=ALU.mult)
        nc.vector.tensor_scalar(out=cmask[:, W:P], in0=w2[:, 1:2].to_broadcast([P, W]), scalar1=NEG, scalar2=None, op0=ALU.mult)
        maskj = const.tile([P, H], F32, name="maskj")
        nc.vector.tensor_scalar(out=maskj[:], in0=w2[:, 0:H], scalar1=NEG, scalar2=None, op0=ALU.mult)
        warm_in = const.tile([P, 1], F32, name="warm_in")
        warm_out = const.tile([P, 1], F32, name="warm_out")
        nc.vector.memset(warm_in[:], 0.0)
        nc.scalar.activation(out=warm_out[:], in_=warm_in[:], func=ACT.Exp)

        natq, natk, nats = [], [], []
        for b in range(RING):
            tq = keep.tile([P, NATW], I32, name="natq%d" % b, align_bytes=64)
            tk = keep.tile([P, NATKW], I32, name="natk%d" % b, align_bytes=64)
            ts = keep.tile([P, NATKW], U8, name="nats%d" % b, align_bytes=64)
            natq.append(tq)
            natk.append(tk)
            nats.append(ts)

        def init_ring(b):
            sv = nats[b][:].bitcast(I32)
            nc.vector.memset(natq[b][:, W:NATW].rearrange("p (u x w) -> p u x w", x=3, w=W)[:, :, 1, :], 0)
            nc.vector.memset(sv[:, 0 : W // 4], 0)
            nc.vector.memset(natk[b][:, 0:W], 0)

        init_ring(0)
        init_ring(1)
        movq = keep.tile([P, MOVW], I32, name="movq", align_bytes=64)
        movk = keep.tile([P, MOVW], I32, name="movk", align_bytes=64)
        movs = keep.tile([P, MOVW], U8, name="movs", align_bytes=64)
        nc.vector.memset(movq[:, H * W : MOVW], 0)
        nc.vector.memset(movk[:, H * W : MOVW], 0)
        nc.vector.memset(movs[:, H * W : MOVW].bitcast(I32), 0)
        s2 = keep.tile([P, H * W], F32, name="s2")
        s2v = s2[:].rearrange("p (h w) -> p h w", w=W)

        raws = {}
        gs = {}
        prob = {}
        banks = {}
        sums = {}
        recs = {}

        def load(t):
            n, c = divmod(t, NCHUNK)
            for nm in ("q", "k"):
                raws[(t, nm)] = rawp.tile([P, 4, CH], BF16, name="raw", tag="raw")
            pieces = (0, 3, 1, 2) if t == 0 else (0,)
            pw = CH // len(pieces)
            for i in pieces:
                for nm, src in (("q", qv), ("k", kv)):
                    nc.sync.dma_start(out=raws[(t, nm)][:, :, i * pw : (i + 1) * pw], in_=src[n, :, :, c * CH + i * pw : c * CH + (i + 1) * pw])

        def interleave(t):
            xv = XV0 if t == 0 else (XV1 if t <= NCHUNK + 1 else XV)
            step = 256 if t == 0 else CH
            for nm in ("q", "k"):
                gs[(t, nm)] = gp.tile([P, 4 * CH], BF16, name="g", tag="g", align_bytes=64)
            for a in range(0, CH, step):
                for nm in ("q", "k"):
                    gv = gs[(t, nm)][:].rearrange("p (c i y z) -> p c y i z", i=8, y=2, z=2)
                    rv = raws[(t, nm)][:].rearrange("p (y z) (c i) -> p c y i z", i=8, z=2)
                    b = min(a + step, CH)
                    if a < xv:
                        nc.vector.tensor_copy(out=gv[:, a // 8 : min(b, xv) // 8, :, :, :], in_=rv[:, a // 8 : min(b, xv) // 8, :, :, :])
                    if b > xv:
                        nc.scalar.copy(out=gv[:, max(a, xv) // 8 : b // 8, :, :, :], in_=rv[:, max(a, xv) // 8 : b // 8, :, :, :])

        def quantise(t):
            b = t % RING
            rw = 4 * W
            gq = gs[(t, "q")]
            gk = gs[(t, "k")]
            mid = [(2 * u + 1, 2, W + TRI * u + 2 * W) for u in range(ROWS // 2 - 1)]
            for r0, nr, pos in [(0, 1, W)] + mid + [(ROWS - 1, 1, NATW - W)]:
                nc.vector.quantize_mx(
                    out=natq[b][:, pos : pos + nr * W].bitcast(FP8X4),
                    scales=nats[b][:, W + r0 * W : W + (r0 + nr) * W],
                    in_=gq[:, r0 * rw : (r0 + nr) * rw],
                )
            nr = ROWS // 2
            for r0 in (0, nr):
                nc.vector.quantize_mx(
                    out=natk[b][:, W + r0 * W : W + (r0 + nr) * W].bitcast(FP8X4),
                    scales=nats[b][4:P, W + r0 * W : W + (r0 + nr) * W],
                    in_=gk[:, r0 * rw : (r0 + nr) * rw],
                )

        def moves(t):
            c = t % NCHUNK
            b = t % RING
            h0 = c * ROWS
            wstep = W // 4 if t == NSTEP - 1 else W
            for w0 in range(0, W, wstep):
                for src, dst in ((natq[b], movq), (natk[b], movk), (nats[b], movs)):
                    if dst is not movq:
                        sv = src[:, W:NATKW].rearrange("p (u v w) -> p u v w", u=ROWS // 2, v=2)[:, :, :, w0 : w0 + wstep]
                    else:
                        sv = src[:, W:NATW].rearrange("p (u x w) -> p u x w", u=ROWS // 2, x=3)[:, :, 0:3:2, w0 : w0 + wstep]
                    dv = dst[:, 0 : H * W].rearrange("p (w h) -> p w h", h=H)[:, w0 : w0 + wstep, h0 : h0 + ROWS]
                    if dst is movs:
                        nc.vector.tensor_copy(
                            out=dv.rearrange("p (a i) (g r) -> p a g i r", i=4, g=8),
                            in_=src[:, W:NATKW].rearrange("p (g r w) -> p g r w", g=8, r=2)[:, :, :, w0 : w0 + wstep].rearrange("p g r (a i) -> p a g i r", i=4),
                        )
                    else:
                        nc.vector.tensor_copy(
                            out=dv.rearrange("p (a i) (u v) -> p a u i v", i=4, v=2),
                            in_=sv.rearrange("p u v (a i) -> p a u i v", i=4),
                        )

        def col_energies(n):
            for wq in range(W // 4):
                eh = psum.tile([P, 4, P], F32, name="eh", tag="bank")
                if wq == 0:
                    b = (n * NCHUNK + NCHUNK - 1) % RING
                    bo = (b - 1) % RING
                    for d in range(WARM):
                        nc.tensor.matmul_mx(
                            out=eh[:, d % 4, :],
                            lhsT=natq[b][:, W : W + P].bitcast(FP8X4),
                            lhsT_scale=nats[bo][:, W : W + P],
                            rhs=natk[bo][:, W : W + P].bitcast(FP8X4),
                            rhs_scale=nats[bo][4:P, W : W + P],
                            start=True,
                            stop=True,
                        )
                for i in range(4):
                    a = (4 * wq + i) * H
                    nc.tensor.matmul_mx(
                        out=eh[:, i, :],
                        lhsT=movk[:, a : a + P].bitcast(FP8X4),
                        lhsT_scale=movs[4:P, a : a + P],
                        rhs=movq[:, a : a + P].bitcast(FP8X4),
                        rhs_scale=movs[:, a : a + P],
                        start=True,
                        stop=True,
                    )
                if n == NH - 1:
                    nc.vector.tensor_tensor(
                        out=s2v[:, :, 4 * wq : 4 * wq + 4],
                        in0=eh[:, :, 0:H].rearrange("p w h -> p h w"),
                        in1=maskj[:].unsqueeze(2).to_broadcast([P, H, 4]),
                        op=ALU.add,
                    )
                else:
                    nc.scalar.copy(out=s2v[:, :, 4 * wq : 4 * wq + 4], in_=eh[:, :, 0:H].rearrange("p w h -> p h w"))

        def bank_rows(n, bk):
            s0 = 3 * bk
            ns = min(3, H // 2 - s0)
            ps = psum.tile([P, 4 * P], F32, name="ps", tag="bank")
            banks[(n, bk)] = ps
            for i in reversed(range(ns)):
                s = s0 + i
                b = (n * NCHUNK + s // (ROWS // 2)) % RING
                a = W + TRI * (s % (ROWS // 2))
                ka = 2 * W * (s % (ROWS // 2))
                o = 3 * W + W * i
                nc.tensor.matmul_mx(
                    out=ps[:, o : o + P],
                    lhsT=natq[b][:, a : a + P].bitcast(FP8X4),
                    lhsT_scale=nats[b][:, ka + W : ka + W + P],
                    rhs=natk[b][:, ka : ka + P].bitcast(FP8X4),
                    rhs_scale=nats[b][4:P, ka : ka + P],
                    start=True,
                    stop=False,
                )
                nc.tensor.matmul_mx(
                    out=ps[:, o : o + P],
                    lhsT=natq[b][:, a + W : a + W + P].bitcast(FP8X4),
                    lhsT_scale=nats[b][:, ka + W : ka + W + P],
                    rhs=natk[b][:, ka + W : ka + W + P].bitcast(FP8X4),
                    rhs_scale=nats[b][4:P, ka + W : ka + W + P],
                    start=False,
                    stop=True,
                )

        def bank_rest(n, bk):
            s0 = 3 * bk
            ns = min(3, H // 2 - s0)
            ps = banks[(n, bk)]
            for i in range(ns):
                s = s0 + i
                if n == NH - 1:
                    nc.tensor.transpose(ps[:, W * i : W * i + P], s2[:, P * s : P * (s + 1)], w2[:, 0:P])
                else:
                    nc.tensor.matmul(out=ps[:, W * i : W * i + P], lhsT=s2[:, P * s : P * (s + 1)], rhs=w2[:, 0:P], is_transpose=True, start=True, stop=False)
                    nc.tensor.matmul(out=ps[:, W * i : W * i + P], lhsT=cmask[:], rhs=w2[:, P - 2 * s : 2 * P - 2 * s], is_transpose=True, start=False, stop=True)
            pv = ps[:].rearrange("p (c x j) -> p c x j", c=2, x=4)
            if bk % 2 == 0:
                prob[(n, bk // 2)] = pp.tile([P, 6, P], F32, name="prob", tag="prob")
            if bk == 0:
                sums[n] = stat.tile([P, H // 2], F32, name="sums", tag="sums", bufs=2)
            pt = prob[(n, bk // 2)]
            o = 3 * (bk % 2)
            nm = stat.tile([P, 4], F32, name="nm", tag="nm")
            nc.vector.tensor_reduce(out=nm[:, 0:ns], in_=pv[:, :, 0:ns, :].rearrange("p c x j -> p x c j"), axis=AX.XY, op=ALU.max, negate=True)
            for i in range(ns):
                nc.scalar.activation(
                    out=pt[:, o + i, :].rearrange("p (c j) -> p c j", c=2),
                    in_=pv[:, :, i, :],
                    func=ACT.Exp,
                    bias=nm[:, i : i + 1],
                    scale=1.0,
                    accum_out=sums[n][:, s0 + i : s0 + i + 1],
                )

        def pair_recip(n, pr):
            first = 6 * pr
            cnt = min(6, H // 2 - first)
            if pr == 0:
                recs[n] = stat.tile([P, H // 2], F32, name="recs", tag="recs", bufs=2)
            nc.vector.reciprocal(out=recs[n][:, first : first + cnt], in_=sums[n][:, first : first + cnt])

        def pair_out(n, pr):
            first = 6 * pr
            cnt = min(6, H // 2 - first)
            pt = prob[(n, pr)]
            for i in range(cnt):
                if n == NH - 1:
                    nc.vector.tensor_scalar(out=pt[:, i, :], in0=pt[:, i, :], scalar1=recs[n][:, first + i : first + i + 1], scalar2=None, op0=ALU.mult)
                else:
                    nc.scalar.activation(out=pt[:, i, :], in_=pt[:, i, :], func=ACT.Copy, scale=recs[n][:, first + i : first + i + 1])
            nc.sync.dma_start(out=o0v[n, :, first : first + cnt, :], in_=pt[:, 0:cnt, :])
            f8 = f8p.tile([P, 6, P], FP8, name="f8", tag="f8")
            if n == 1:
                nc.scalar.activation(out=f8[:, 0:cnt, :], in_=pt[:, 0:cnt, :], func=ACT.Copy, scale=Y_SCALE, saturate=False)
            else:
                nc.vector.tensor_scalar(out=f8[:, 0:cnt, :], in0=pt[:, 0:cnt, :], scalar1=Y_SCALE, scalar2=None, op0=ALU.mult, saturate=False)
            for a in range(0, cnt, 3):
                e = min(a + 3, cnt)
                nc.sync.dma_start(out=o1v[n, :, first + a : first + e, :], in_=f8[:, a:e, :].bitcast(U8))

        load(0)
        load(1)
        interleave(0)
        for b in range(2, RING):
            init_ring(b)
        load(2)
        interleave(1)
        plan = {0: (0, 1, 2, 3), 1: (4, 5, 6, 7), 2: (8, 9, 10)}
        for t in range(NSTEP):
            if t + 3 < NSTEP:
                load(t + 3)
            if t + 2 < NSTEP:
                interleave(t + 2)
            quantise(t)
            moves(t)
            n, e = divmod(t, NCHUNK)
            if t == NSTEP - 1:
                for bk in range(AHEAD):
                    bank_rows(n, bk)
            if e == NCHUNK - 1:
                col_energies(n)
            if t == NSTEP - 1:
                for pr in range(6):
                    pair_out(1, pr)
            if n >= 1:
                for bk in plan.get(e, ()):
                    bank_rows(n - 1, bk)
                    bank_rest(n - 1, bk)
                    if bk % 2 == 1 or bk == 10:
                        pair_recip(n - 1, bk // 2)
                        if n == 1:
                            pair_out(0, bk // 2)
        for bk in range(11):
            if bk + AHEAD < 11:
                bank_rows(NH - 1, bk + AHEAD)
            bank_rest(NH - 1, bk)
            if bk % 2 == 1 or bk == 10:
                pair_recip(NH - 1, bk // 2)
                pair_out(NH - 1, bk // 2)
